import numpy as np
import ml_dtypes


def mxq(x, axis, fmt="e4m3"):
    dtype, down = {"e4m3": (ml_dtypes.float8_e4m3fn, 7), "e5m2": (ml_dtypes.float8_e5m2, 14)}[fmt]
    v = np.moveaxis(np.asarray(x, np.float32).astype(ml_dtypes.bfloat16).astype(np.float64), axis, -1)
    blocks = v.reshape(v.shape[:-1] + (-1, 32))
    amax = np.abs(blocks).max(-1, keepdims=True)
    byte = np.maximum(np.where(amax > 0, np.frexp(amax)[1] - 1 + 127, 0) - down, 1)
    scale = np.exp2(byte - 127.0)
    codes = (blocks / scale).astype(np.float32).astype(dtype).astype(np.float64)
    return np.moveaxis((codes * scale).reshape(v.shape), -1, axis)


WIDE = False


def mx_kscale(k):
    if not WIDE:
        return np.ones(k)
    levels = np.array([10, -10, 5, -5, 0])
    if k % 512:
        return np.exp2(np.random.permutation(np.resize(levels, k // 32))).repeat(32)
    a = np.empty((k // 512, 16))
    for p in range(k // 512):
        a[p, :8] = np.random.permutation(np.resize(levels, 8))
        for g in range(8):
            far = levels[np.abs(levels - a[p, g]) >= 10]
            a[p, g + 8] = far[np.random.randint(len(far))]
    return np.exp2(a.ravel()).repeat(32)


BF16 = ml_dtypes.bfloat16


def bf(x):
    return np.asarray(x, np.float32).astype(BF16)


def f64(x):
    return np.asarray(x).astype(np.float64)


B, D_IN, D_OUT = 1024, 1024, 1024


def sigmoid(v):
    return 1.0 / (1.0 + np.exp(-v))


def setup_inputs():
    s, t = mx_kscale(D_IN), mx_kscale(D_OUT)

    def wx():
        return bf(np.random.standard_normal((D_IN, D_OUT)) / np.sqrt(D_IN) / s[:, None])

    def wh():
        return bf(np.random.standard_normal((D_OUT, D_OUT)) / np.sqrt(D_OUT) / t[:, None])

    return {"x": bf(np.random.standard_normal((B, D_IN)) * s),
            "hist": bf(np.random.standard_normal((B, D_OUT)) * t),
            "Wix": wx(), "Wih": wh(), "b_i": bf(np.random.standard_normal(D_OUT) * 0.3),
            "Wcx": wx(), "Wch": wh(), "b_c": bf(np.random.standard_normal(D_OUT) * 0.3)}


def reference(x, hist, Wix, Wih, b_i, Wcx, Wch, b_c):
    xq = mxq(f64(x), 1, "e4m3")
    hq = mxq(f64(hist), 1, "e4m3")
    i = sigmoid((xq @ mxq(f64(Wix), 0, "e4m3")) + (hq @ mxq(f64(Wih), 0, "e4m3")) + f64(b_i))
    g = np.tanh((xq @ mxq(f64(Wcx), 0, "e4m3")) + (hq @ mxq(f64(Wch), 0, "e4m3")) + f64(b_c))
    return i * g

@@ -1,0 +1,320 @@
+from contextlib import ExitStack
+
+import concourse.mybir as mybir
+from concourse.masks import make_identity
+
+F32 = mybir.dt.float32
+BF16 = mybir.dt.bfloat16
+U32 = mybir.dt.uint32
+U8 = mybir.dt.uint8
+I32 = mybir.dt.int32
+FP8X4 = mybir.dt.float8_e4m3fn_x4
+ACT = mybir.ActivationFunctionType
+ALU = mybir.AluOpType
+
+P = 128
+BANK = 512
+FLOPS = 2 * 1024 * 2048 * 2048
+
+REGROUP_AT = {
+    (1, 0): (0, "S"), (1, 1): (0, "VS"), (2, 0): (4, "V"), (2, 1): (4, "VS"), (3, 0): (17, "VS"), (3, 1): (13, "V"),
+    (4, 0): (17, "VS"), (4, 1): (18, "VS"), (5, 0): (23, "V"), (5, 1): (18, "S"), (6, 0): (32, "S"), (6, 1): (33, "S"),
+    (7, 0): (33, "V"), (7, 1): (30, "V"),
+}
+QUANT_AT = {
+    (1, 0): 0, (1, 1): 1, (2, 0): 4, (2, 1): 14, (3, 0): 18, (3, 1): 16, (4, 0): 21, (4, 1): 23, (5, 0): 25, (5, 1): 25,
+    (6, 0): 36, (6, 1): 36, (7, 0): 35, (7, 1): 35,
+}
+VECTOR_SHARE = 336
+VECTOR_X_BANKS = (3, 4, 7, 10)
+STEP_2_LAG = 1
+STEP_3_LAG = 3
+TURN_BACK_LAG = 5
+VECTOR_BACK_BANK = 1
+GPSIMD_PRODUCTS = 5
+HALVED_GROUPS = 2
+
+
+def tile_lstmmirrored_pa_kernel(tc, x, hist, Wix, Wih, b_i, Wcx, Wch, b_c, out):
+    nc = tc.nc
+    with ExitStack() as ctx:
+        ctx.enter_context(tc.manual_schedule())
+        const = ctx.enter_context(tc.tile_pool(name="const", bufs=1))
+        keep = ctx.enter_context(tc.tile_pool(name="keep", bufs=1))
+        raw = ctx.enter_context(tc.tile_pool(name="raw", bufs=8))
+        grp = ctx.enter_context(tc.tile_pool(name="grp", bufs=8))
+        spool = ctx.enter_context(tc.tile_pool(name="spool", bufs=12))
+        gpool = ctx.enter_context(tc.tile_pool(name="gpool", bufs=5))
+        upool = ctx.enter_context(tc.tile_pool(name="upool", bufs=4))
+        stpool = ctx.enter_context(tc.tile_pool(name="stpool", bufs=2))
+        psum = ctx.enter_context(tc.psum_pool(name="psum", bufs=8))
+
+        x_rows = x.rearrange("(p t) k -> p (t k)", t=8)
+        hist_rows = hist.rearrange("(p t) k -> p (t k)", t=8)
+        out_rows = out.rearrange("(p t) n -> p t n", t=8)
+        matrices = ((Wix, Wih), (Wcx, Wch))
+        blocks = [(nh, gate, part) for nh in range(2) for gate in range(2) for part in range(2)]
+
+        warm = const.tile([P, 1], F32, name="warm")
+        nc.vector.memset(warm[:], 0.0)
+        nc.scalar.activation(out=warm[:], in_=warm[:], func=ACT.Sigmoid)
+        ident = const.tile([P, P], F32, name="ident")
+        make_identity(nc, ident[:])
+        bias_row = const.tile([P, 2048], BF16, name="bias_row")
+        nc.vector.memset(bias_row[:].bitcast(I32), 0)
+        nc.scalar.dma_start(out=bias_row[0:1, 0:1024], in_=b_i.rearrange("(o n) -> o n", o=1))
+        nc.scalar.dma_start(out=bias_row[0:1, 1024:2048], in_=b_c.rearrange("(o n) -> o n", o=1))
+        ones = const.tile([P, P], BF16, name="ones")
+        nc.vector.memset(ones[:], 1.0)
+        bias_col = const.tile([P, 8], F32, name="bias_col")
+        bias_wide = const.tile([P, 2 * BANK], F32, name="bias_wide")
+
+        x_codes = keep.tile([P, 4 * 1024], U32, name="x_codes", align_bytes=64)
+        x_scales = keep.tile([P, 4 * 1024], U8, name="x_scales", align_bytes=64)
+        w_codes = keep.tile([P, 8 * 1024], U32, name="w_codes", align_bytes=64)
+        w_scales = keep.tile([P, 8 * 1024], U8, name="w_scales", align_bytes=64)
+
+        x_raw = []
+        for si, rows in enumerate((x_rows, hist_rows)):
+            for h in range(2):
+                tile4 = raw.tile([P, 4096], BF16, name="x_raw%d%d" % (si, h), tag="raw")
+                for a in range(2):
+                    lo = (h * 4 + a * 2) * 1024
+                    nc.sync.dma_start(out=tile4[:, a * 2048:(a + 1) * 2048], in_=rows[:, lo:lo + 2048])
+                x_raw.append(tile4)
+
+        w_raw = {}
+
+        def load_weights(k):
+            nh, gate, part = blocks[k]
+            src = matrices[gate][part][:, nh * BANK:(nh + 1) * BANK].rearrange("(g q t) c -> q g t c", g=2, t=4)
+            w_raw[k] = raw.tile([P, 4096], BF16, name="w_raw%d" % k, tag="raw")
+            dst = w_raw[k][:].rearrange("q (g t c) -> q g t c", g=2, t=4)
+            if k < 2:
+                for g in range(2):
+                    for t in (0, 2):
+                        nc.sync.dma_start(out=dst[:, g, t:t + 2, :], in_=src[:, g, t:t + 2, :])
+            else:
+                for g in range(2):
+                    nc.sync.dma_start(out=dst[:, g, :, :], in_=src[:, g, :, :])
+
+        for k in range(4):
+            load_weights(k)
+
+        x_grouped = {}
+
+        def transpose_pair(si, tp):
+            words = x_raw[si * 2 + tp // 2][:].bitcast(F32)
+            h = tp // 2
+            for g in range(2):
+                bank = psum.tile([P, BANK], F32, name="bank_x", tag="bank")
+                for u in range(2):
+                    for t2 in range(2):
+                        w0 = ((tp % 2) * 2 + t2) * 512 + 2 * g * P
+                        o0 = (u * 2 + t2) * P
+                        nc.tensor.transpose(bank[:, o0:o0 + P], words[:, w0 + u:w0 + 2 * P:2], ident[:])
+                c = 2 * si + g
+                if tp % 2 == 0:
+                    x_grouped[(c, h)] = grp.tile([P, 2048], BF16, name="x_grouped%d%d" % (c, h), tag="grp", align_bytes=64)
+                dst = x_grouped[(c, h)][:].bitcast(F32).rearrange("q (c u) -> q c u", u=2)
+                dst = dst[:, (tp % 2) * 256:(tp % 2) * 256 + 256, :]
+                src = bank[:].rearrange("q (u c) -> q c u", u=2)
+                if (si * 8 + tp * 2 + g) in VECTOR_X_BANKS:
+                    nc.vector.tensor_copy(out=dst, in_=src)
+                else:
+                    nc.scalar.copy(out=dst, in_=src)
+
+        def quantise_x(si, h):
+            for g in range(2):
+                c = 2 * si + g
+                lo = c * 1024 + h * BANK
+                nc.vector.quantize_mx(
+                    out=x_codes[:, lo:lo + BANK].bitcast(FP8X4),
+                    scales=x_scales[:, lo:lo + BANK],
+                    in_=x_grouped[(c, h)][:],
+                )
+
+        for si in range(2):
+            for tp in range(4):
+                transpose_pair(si, tp)
+                if (si, tp) in ((0, 2), (1, 0), (1, 2)):
+                    done = si * 4 + tp - 2
+                    quantise_x(done // 4, (done % 4) // 2)
+
+        bank = psum.tile([P, BANK], F32, name="bank_b", tag="bank")
+        for col in range(8):
+            lo = (col // 4) * 1024 + (col % 4) * P
+            nc.tensor.matmul(bank[:, col * 32:(col + 1) * 32], lhsT=bias_row[:, lo:lo + P], rhs=ones[:, 0:32],
+                             start=True, stop=True)
+        nc.scalar.copy(out=bias_col[:], in_=bank[:, 0:256].rearrange("p (c r) -> p c r", r=32)[:, :, 0])
+        for gate in range(2):
+            bank = psum.tile([P, BANK], F32, name="bank_w", tag="bank")
+            lo = gate * 1024 + BANK
+            nc.tensor.matmul(bank[:], lhsT=ones[:], rhs=bias_row[:, lo:lo + BANK], start=True, stop=True)
+            nc.scalar.copy(out=bias_wide[:, gate * BANK:(gate + 1) * BANK], in_=bank[:])
+
+        for k in range(4, 8):
+            load_weights(k)
+
+        w_grouped = {}
+
+        def regroup(k, g, engine, lo=0, cols=BANK):
+            if lo == 0:
+                w_grouped[(k, g)] = grp.tile([P, 2048], BF16, name="w_grouped%d%d" % (k, g), tag="grp", align_bytes=64)
+            dst = w_grouped[(k, g)][:, 4 * lo:4 * (lo + cols)].rearrange("q (c i t) -> q c t i", i=4, t=4)
+            src = w_raw[k][:, g * 2048:(g + 1) * 2048].rearrange("q (t n) -> q t n", t=4)
+            src = src[:, :, lo:lo + cols].rearrange("q t (c i) -> q c t i", i=4)
+            if engine == "S":
+                nc.scalar.copy(out=dst, in_=src)
+            else:
+                nc.vector.tensor_copy(out=dst, in_=src)
+
+        def quantise_w(k, g, lo=0, cols=BANK):
+            nh, gate, part = blocks[k]
+            at = (gate * 4 + part * 2 + g) * 1024 + nh * BANK + lo
+            nc.vector.quantize_mx(
+                out=w_codes[:, at:at + cols].bitcast(FP8X4),
+                scales=w_scales[:, at:at + cols],
+                in_=w_grouped[(k, g)][:, 4 * lo:4 * (lo + cols)],
+            )
+
+        banks = {}
+        sigmoids = {}
+        sums = {}
+        gate_out = {}
+        staged = {}
+
+        def mx_pass(nh, gate, h, i, lo, cols, c):
+            w_at = (gate * 4 + c) * 1024 + nh * BANK
+            if nh == 0:
+                l_at, r_at = w_at + i * P, c * 1024 + h * BANK
+                l_codes, l_scales, r_codes, r_scales = w_codes, w_scales, x_codes, x_scales
+            else:
+                l_at, r_at = c * 1024 + (h * 4 + i) * P, w_at + lo
+                l_codes, l_scales, r_codes, r_scales = x_codes, x_scales, w_codes, w_scales
+            nc.tensor.matmul_mx(
+                out=banks[(h, i, lo)][:, 0:cols],
+                lhsT=l_codes[:, l_at:l_at + P].bitcast(FP8X4),
+                lhsT_scale=l_scales[:, l_at:l_at + P],
+                rhs=r_codes[:, r_at:r_at + cols].bitcast(FP8X4),
+                rhs_scale=r_scales[:, r_at:r_at + cols],
+                start=(c == 0),
+                stop=(c == 3),
+            )
+
+        def store(nh, h, first, count, lo=0, cols=BANK):
+            nc.sync.dma_start(
+                out=out_rows[:, h * 4 + first:h * 4 + first + count, nh * BANK + lo:nh * BANK + lo + cols],
+                in_=staged[h][:, first:first + count, lo:lo + cols],
+            )
+
+        def gate_tile(gate, h, i, lo):
+            if gate == 0:
+                sigmoids[(h, i)] = spool.tile([P, BANK], F32, name="sigmoid", tag="s")
+                gate_out[(h, i, lo)] = sigmoids[(h, i)]
+            else:
+                gate_out[(h, i, lo)] = gpool.tile([P, BANK], F32, name="tanh", tag="gt")
+
+        def step_1(nh, gate, h, i, lo, cols):
+            bank = banks[(h, i, lo)]
+            if nh == 0:
+                gate_tile(gate, h, i, lo)
+                nc.scalar.activation(out=gate_out[(h, i, lo)][:], in_=bank[:], func=ACT.Sigmoid if gate == 0 else ACT.Tanh,
+                                     bias=bias_col[:, 4 * gate + i:4 * gate + i + 1])
+            else:
+                at = gate * BANK + lo
+                sums[(h, i, lo)] = upool.tile([P, BANK], F32, name="sum", tag="u")
+                nc.vector.tensor_tensor(out=sums[(h, i, lo)][:, 0:cols], in0=bank[:, 0:cols],
+                                        in1=bias_wide[:, at:at + cols], op=ALU.add)
+
+        def step_2(nh, gate, h, i, lo, cols):
+            if nh == 0:
+                product = sigmoids[(h, i)]
+                nc.vector.tensor_tensor(out=product[:], in0=product[:], in1=gate_out[(h, i, lo)][:], op=ALU.mult)
+            else:
+                gate_tile(gate, h, i, lo)
+                nc.scalar.activation(out=gate_out[(h, i, lo)][:, 0:cols], in_=sums[(h, i, lo)][:, 0:cols],
+                                     func=ACT.Sigmoid if gate == 0 else ACT.Tanh)
+
+        def step_3(nh, gate, h, i, lo, cols):
+            engine = nc.gpsimd if h * 4 + i < GPSIMD_PRODUCTS else nc.vector
+            engine.tensor_tensor(out=staged[h][:, i, lo:lo + cols], in0=sigmoids[(h, i)][:, lo:lo + cols],
+                                 in1=gate_out[(h, i, lo)][:, 0:cols], op=ALU.mult)
+            store(nh, h, i, 1, lo, cols)
+
+        def turn_back(nh, h):
+            for tl in range(4):
+                bank = psum.tile([P, BANK], F32, name="bank_t", tag="bank")
+                for i in range(4):
+                    nc.tensor.transpose(bank[:, i * P:(i + 1) * P], sigmoids[(h, i)][:, tl * P:(tl + 1) * P], ident[:])
+                if tl == VECTOR_BACK_BANK:
+                    nc.vector.tensor_copy(out=staged[h][:, tl, :], in_=bank[:])
+                else:
+                    nc.scalar.copy(out=staged[h][:, tl, :], in_=bank[:])
+                if tl % 2 == 1:
+                    store(nh, h, tl - 1, 2)
+
+        pairs = [(h, i) for h in range(2) for i in range(4)]
+        visits = []
+        for nh in range(2):
+            for gate in range(2):
+                if nh == 0:
+                    for part in range(2):
+                        for h, i in pairs:
+                            visits.append(((nh, gate, h, i, 0, BANK), (2 * part, 2 * part + 1)))
+                else:
+                    for h, i in pairs:
+                        if gate == 1 and h * 4 + i >= 8 - HALVED_GROUPS:
+                            visits.append(((nh, gate, h, i, 0, 256), (0, 1, 2, 3)))
+                            visits.append(((nh, gate, h, i, 256, 256), (0, 1, 2, 3)))
+                        else:
+                            visits.append(((nh, gate, h, i, 0, BANK), (0, 1, 2, 3)))
+        later = {}
+
+        def defer(n, step, args):
+            later[n] = later.get(n, []) + [(step, args)]
+
+        for g in range(2):
+            for lo in (0, 256):
+                regroup(0, g, "V", lo, 256)
+                quantise_w(0, g, lo, 256)
+        quantise_x(1, 1)
+
+        sub_blocks = [(k, g) for k in range(1, 8) for g in range(2)]
+        for n in range(len(visits) + TURN_BACK_LAG + 1):
+            for k, g in sub_blocks:
+                if REGROUP_AT[(k, g)][0] == n:
+                    if REGROUP_AT[(k, g)][1] == "VS":
+                        regroup(k, g, "V", 0, VECTOR_SHARE)
+                        regroup(k, g, "S", VECTOR_SHARE, BANK - VECTOR_SHARE)
+                    else:
+                        regroup(k, g, REGROUP_AT[(k, g)][1])
+            for k, g in sub_blocks:
+                if QUANT_AT[(k, g)] == n:
+                    quantise_w(k, g)
+            if n < len(visits):
+                group, passes = visits[n]
+                nh, gate, h, i, lo, cols = group
+                if passes == (0, 1):
+                    if (h, i) == (0, 0):
+                        for h2, i2 in pairs:
+                            banks[(h2, i2, 0)] = psum.tile([P, BANK], F32, name="bank_g", tag="bank")
+                        for c in passes:
+                            for h2, i2 in sorted(pairs, key=lambda hi: hi[1] // 2):
+                                mx_pass(nh, gate, h2, i2, 0, BANK, c)
+                else:
+                    if passes[0] == 0:
+                        banks[(h, i, lo)] = psum.tile([P, BANK], F32, name="bank_g", tag="bank")
+                    if gate == 1 and i == 0:
+                        staged[h] = stpool.tile([P, 4, BANK], F32, name="staged", tag="st")
+                    for c in passes:
+                        mx_pass(nh, gate, h, i, lo, cols, c)
+                    step_1(*group)
+                    if nh == 1 or gate == 1:
+                        defer(n + STEP_2_LAG, step_2, group)
+                    if nh == 1 and gate == 1:
+                        defer(n + STEP_3_LAG, step_3, group)
+                    if nh == 0 and gate == 1 and i == 3:
+                        defer(n + TURN_BACK_LAG, turn_back, (nh, h))
+            for step, args in later.get(n, []):
+                step(*args)

@@ -26,13 +26,13 @@ QUANT_AT = {
     (6, 0): 36, (6, 1): 36, (7, 0): 35, (7, 1): 35,
 }
 VECTOR_SHARE = 336
-VECTOR_X_BANKS = (3, 4, 7, 10)
+VECTOR_X_BANKS = (3, 7, 10, 12, 14)
 STEP_2_LAG = 1
-STEP_3_LAG = 3
+STEP_3_LAG = 2
 TURN_BACK_LAG = 5
 VECTOR_BACK_BANK = 1
-GPSIMD_PRODUCTS = 5
-HALVED_GROUPS = 2
+GPSIMD_PRODUCTS = 3
+HALVED_GROUPS = 3
 
 
 def tile_lstmmirrored_pa_kernel(tc, x, hist, Wix, Wih, b_i, Wcx, Wch, b_c, out):
@@ -69,11 +69,22 @@ def tile_lstmmirrored_pa_kernel(tc, x, hist, Wix, Wih, b_i, Wcx, Wch, b_c, out):
         bias_col = const.tile([P, 8], F32, name="bias_col")
         bias_wide = const.tile([P, 2 * BANK], F32, name="bias_wide")
 
-        x_codes = keep.tile([P, 4 * 1024], U32, name="x_codes", align_bytes=64)
-        x_scales = keep.tile([P, 4 * 1024], U8, name="x_scales", align_bytes=64)
-        w_codes = keep.tile([P, 8 * 1024], U32, name="w_codes", align_bytes=64)
-        w_scales = keep.tile([P, 8 * 1024], U8, name="w_scales", align_bytes=64)
+        x_codes = keep.tile([P, 4 * 1024], U32, name="x_codes", align_bytes=256)
+        x_scales = keep.tile([P, 4 * 1024], U8, name="x_scales", align_bytes=256)
+        w_codes = keep.tile([P, 8 * 1024], U32, name="w_codes", align_bytes=256)
+        w_scales = keep.tile([P, 8 * 1024], U8, name="w_scales", align_bytes=256)
 
+        w_raw = {}
+
+        def load_weights(k):
+            nh, gate, part = blocks[k]
+            src = matrices[gate][part][:, nh * BANK:(nh + 1) * BANK].rearrange("(g q t) c -> q g t c", g=2, t=4)
+            w_raw[k] = raw.tile([P, 4096], BF16, name="w_raw%d" % k, tag="raw")
+            dst = w_raw[k][:].rearrange("q (g t c) -> q g t c", g=2, t=4)
+            for g in range(2):
+                nc.sync.dma_start(out=dst[:, g, :, :], in_=src[:, g, :, :])
+
+        load_weights(0)
         x_raw = []
         for si, rows in enumerate((x_rows, hist_rows)):
             for h in range(2):
@@ -83,23 +94,35 @@ def tile_lstmmirrored_pa_kernel(tc, x, hist, Wix, Wih, b_i, Wcx, Wch, b_c, out):
                     nc.sync.dma_start(out=tile4[:, a * 2048:(a + 1) * 2048], in_=rows[:, lo:lo + 2048])
                 x_raw.append(tile4)
 
-        w_raw = {}
-
-        def load_weights(k):
-            nh, gate, part = blocks[k]
-            src = matrices[gate][part][:, nh * BANK:(nh + 1) * BANK].rearrange("(g q t) c -> q g t c", g=2, t=4)
-            w_raw[k] = raw.tile([P, 4096], BF16, name="w_raw%d" % k, tag="raw")
-            dst = w_raw[k][:].rearrange("q (g t c) -> q g t c", g=2, t=4)
-            if k < 2:
-                for g in range(2):
-                    for t in (0, 2):
-                        nc.sync.dma_start(out=dst[:, g, t:t + 2, :], in_=src[:, g, t:t + 2, :])
-            else:
-                for g in range(2):
-                    nc.sync.dma_start(out=dst[:, g, :, :], in_=src[:, g, :, :])
-
-        for k in range(4):
+        for k in range(1, 4):
             load_weights(k)
+
+        w_grouped = {}
+
+        def regroup(k, g, engine, lo=0, cols=BANK):
+            if lo == 0:
+                w_grouped[(k, g)] = grp.tile([P, 2048], BF16, name="w_grouped%d%d" % (k, g), tag="grp", align_bytes=64)
+            dst = w_grouped[(k, g)][:, 4 * lo:4 * (lo + cols)].rearrange("q (c i t) -> q c t i", i=4, t=4)
+            src = w_raw[k][:, g * 2048:(g + 1) * 2048].rearrange("q (t n) -> q t n", t=4)
+            src = src[:, :, lo:lo + cols].rearrange("q t (c i) -> q c t i", i=4)
+            if engine == "S":
+                nc.scalar.copy(out=dst, in_=src)
+            else:
+                nc.vector.tensor_copy(out=dst, in_=src)
+
+        def quantise_w(k, g, lo=0, cols=BANK):
+            nh, gate, part = blocks[k]
+            at = (gate * 4 + part * 2 + g) * 1024 + nh * BANK + lo
+            nc.vector.quantize_mx(
+                out=w_codes[:, at:at + cols].bitcast(FP8X4),
+                scales=w_scales[:, at:at + cols],
+                in_=w_grouped[(k, g)][:, 4 * lo:4 * (lo + cols)],
+            )
+
+        for g in range(2):
+            regroup(0, g, "V")
+        for g in range(2):
+            quantise_w(0, g)
 
         x_grouped = {}
 
@@ -134,49 +157,30 @@ def tile_lstmmirrored_pa_kernel(tc, x, hist, Wix, Wih, b_i, Wcx, Wch, b_c, out):
                     in_=x_grouped[(c, h)][:],
                 )
 
+        def biases():
+            bank = psum.tile([P, BANK], F32, name="bank_b", tag="bank")
+            for col in range(8):
+                lo = (col // 4) * 1024 + (col % 4) * P
+                nc.tensor.matmul(bank[:, col * 32:(col + 1) * 32], lhsT=bias_row[:, lo:lo + P], rhs=ones[:, 0:32],
+                                 start=True, stop=True)
+            nc.scalar.copy(out=bias_col[:], in_=bank[:, 0:256].rearrange("p (c r) -> p c r", r=32)[:, :, 0])
+            for gate in range(2):
+                bank = psum.tile([P, BANK], F32, name="bank_w", tag="bank")
+                lo = gate * 1024 + BANK
+                nc.tensor.matmul(bank[:], lhsT=ones[:], rhs=bias_row[:, lo:lo + BANK], start=True, stop=True)
+                nc.scalar.copy(out=bias_wide[:, gate * BANK:(gate + 1) * BANK], in_=bank[:])
+
         for si in range(2):
+            if si == 1:
+                biases()
             for tp in range(4):
                 transpose_pair(si, tp)
                 if (si, tp) in ((0, 2), (1, 0), (1, 2)):
                     done = si * 4 + tp - 2
                     quantise_x(done // 4, (done % 4) // 2)
 
-        bank = psum.tile([P, BANK], F32, name="bank_b", tag="bank")
-        for col in range(8):
-            lo = (col // 4) * 1024 + (col % 4) * P
-            nc.tensor.matmul(bank[:, col * 32:(col + 1) * 32], lhsT=bias_row[:, lo:lo + P], rhs=ones[:, 0:32],
-                             start=True, stop=True)
-        nc.scalar.copy(out=bias_col[:], in_=bank[:, 0:256].rearrange("p (c r) -> p c r", r=32)[:, :, 0])
-        for gate in range(2):
-            bank = psum.tile([P, BANK], F32, name="bank_w", tag="bank")
-            lo = gate * 1024 + BANK
-            nc.tensor.matmul(bank[:], lhsT=ones[:], rhs=bias_row[:, lo:lo + BANK], start=True, stop=True)
-            nc.scalar.copy(out=bias_wide[:, gate * BANK:(gate + 1) * BANK], in_=bank[:])
-
         for k in range(4, 8):
             load_weights(k)
-
-        w_grouped = {}
-
-        def regroup(k, g, engine, lo=0, cols=BANK):
-            if lo == 0:
-                w_grouped[(k, g)] = grp.tile([P, 2048], BF16, name="w_grouped%d%d" % (k, g), tag="grp", align_bytes=64)
-            dst = w_grouped[(k, g)][:, 4 * lo:4 * (lo + cols)].rearrange("q (c i t) -> q c t i", i=4, t=4)
-            src = w_raw[k][:, g * 2048:(g + 1) * 2048].rearrange("q (t n) -> q t n", t=4)
-            src = src[:, :, lo:lo + cols].rearrange("q t (c i) -> q c t i", i=4)
-            if engine == "S":
-                nc.scalar.copy(out=dst, in_=src)
-            else:
-                nc.vector.tensor_copy(out=dst, in_=src)
-
-        def quantise_w(k, g, lo=0, cols=BANK):
-            nh, gate, part = blocks[k]
-            at = (gate * 4 + part * 2 + g) * 1024 + nh * BANK + lo
-            nc.vector.quantize_mx(
-                out=w_codes[:, at:at + cols].bitcast(FP8X4),
-                scales=w_scales[:, at:at + cols],
-                in_=w_grouped[(k, g)][:, 4 * lo:4 * (lo + cols)],
-            )
 
         banks = {}
         sigmoids = {}
@@ -274,10 +278,6 @@ def tile_lstmmirrored_pa_kernel(tc, x, hist, Wix, Wih, b_i, Wcx, Wch, b_c, out):
         def defer(n, step, args):
             later[n] = later.get(n, []) + [(step, args)]
 
-        for g in range(2):
-            for lo in (0, 256):
-                regroup(0, g, "V", lo, 256)
-                quantise_w(0, g, lo, 256)
         quantise_x(1, 1)
 
         sub_blocks = [(k, g) for k in range(1, 8) for g in range(2)]

from contextlib import ExitStack

import concourse.mybir as mybir
from concourse.masks import make_identity

F32 = mybir.dt.float32
BF16 = mybir.dt.bfloat16
U32 = mybir.dt.uint32
U8 = mybir.dt.uint8
I32 = mybir.dt.int32
FP8X4 = mybir.dt.float8_e4m3fn_x4
ACT = mybir.ActivationFunctionType
ALU = mybir.AluOpType

P = 128
BANK = 512
FLOPS = 2 * 1024 * 2048 * 2048

REGROUP_AT = {
    (1, 0): (0, "S"), (1, 1): (0, "VS"), (2, 0): (4, "V"), (2, 1): (4, "VS"), (3, 0): (17, "VS"), (3, 1): (13, "V"),
    (4, 0): (17, "VS"), (4, 1): (18, "VS"), (5, 0): (23, "V"), (5, 1): (18, "S"), (6, 0): (32, "S"), (6, 1): (33, "S"),
    (7, 0): (33, "V"), (7, 1): (30, "V"),
}
QUANT_AT = {
    (1, 0): 0, (1, 1): 1, (2, 0): 4, (2, 1): 14, (3, 0): 18, (3, 1): 16, (4, 0): 21, (4, 1): 23, (5, 0): 25, (5, 1): 25,
    (6, 0): 36, (6, 1): 36, (7, 0): 35, (7, 1): 35,
}
VECTOR_SHARE = 336
VECTOR_X_BANKS = (3, 7, 10, 12, 14)
STEP_2_LAG = 1
STEP_3_LAG = 2
TURN_BACK_LAG = 5
VECTOR_BACK_BANK = 1
GPSIMD_PRODUCTS = 3
HALVED_GROUPS = 3


def tile_lstmmirrored_pa_kernel(tc, x, hist, Wix, Wih, b_i, Wcx, Wch, b_c, out):
    nc = tc.nc
    with ExitStack() as ctx:
        ctx.enter_context(tc.manual_schedule())
        const = ctx.enter_context(tc.tile_pool(name="const", bufs=1))
        keep = ctx.enter_context(tc.tile_pool(name="keep", bufs=1))
        raw = ctx.enter_context(tc.tile_pool(name="raw", bufs=8))
        grp = ctx.enter_context(tc.tile_pool(name="grp", bufs=8))
        spool = ctx.enter_context(tc.tile_pool(name="spool", bufs=12))
        gpool = ctx.enter_context(tc.tile_pool(name="gpool", bufs=5))
        upool = ctx.enter_context(tc.tile_pool(name="upool", bufs=4))
        stpool = ctx.enter_context(tc.tile_pool(name="stpool", bufs=2))
        psum = ctx.enter_context(tc.psum_pool(name="psum", bufs=8))

        x_rows = x.rearrange("(p t) k -> p (t k)", t=8)
        hist_rows = hist.rearrange("(p t) k -> p (t k)", t=8)
        out_rows = out.rearrange("(p t) n -> p t n", t=8)
        matrices = ((Wix, Wih), (Wcx, Wch))
        blocks = [(nh, gate, part) for nh in range(2) for gate in range(2) for part in range(2)]

        warm = const.tile([P, 1], F32, name="warm")
        nc.vector.memset(warm[:], 0.0)
        nc.scalar.activation(out=warm[:], in_=warm[:], func=ACT.Sigmoid)
        ident = const.tile([P, P], F32, name="ident")
        make_identity(nc, ident[:])
        bias_row = const.tile([P, 2048], BF16, name="bias_row")
        nc.vector.memset(bias_row[:].bitcast(I32), 0)
        nc.scalar.dma_start(out=bias_row[0:1, 0:1024], in_=b_i.rearrange("(o n) -> o n", o=1))
        nc.scalar.dma_start(out=bias_row[0:1, 1024:2048], in_=b_c.rearrange("(o n) -> o n", o=1))
        ones = const.tile([P, P], BF16, name="ones")
        nc.vector.memset(ones[:], 1.0)
        bias_col = const.tile([P, 8], F32, name="bias_col")
        bias_wide = const.tile([P, 2 * BANK], F32, name="bias_wide")

        x_codes = keep.tile([P, 4 * 1024], U32, name="x_codes", align_bytes=256)
        x_scales = keep.tile([P, 4 * 1024], U8, name="x_scales", align_bytes=256)
        w_codes = keep.tile([P, 8 * 1024], U32, name="w_codes", align_bytes=256)
        w_scales = keep.tile([P, 8 * 1024], U8, name="w_scales", align_bytes=256)

        w_raw = {}

        def load_weights(k):
            nh, gate, part = blocks[k]
            src = matrices[gate][part][:, nh * BANK:(nh + 1) * BANK].rearrange("(g q t) c -> q g t c", g=2, t=4)
            w_raw[k] = raw.tile([P, 4096], BF16, name="w_raw%d" % k, tag="raw")
            dst = w_raw[k][:].rearrange("q (g t c) -> q g t c", g=2, t=4)
            for g in range(2):
                nc.sync.dma_start(out=dst[:, g, :, :], in_=src[:, g, :, :])

        load_weights(0)
        x_raw = []
        for si, rows in enumerate((x_rows, hist_rows)):
            for h in range(2):
                tile4 = raw.tile([P, 4096], BF16, name="x_raw%d%d" % (si, h), tag="raw")
                for a in range(2):
                    lo = (h * 4 + a * 2) * 1024
                    nc.sync.dma_start(out=tile4[:, a * 2048:(a + 1) * 2048], in_=rows[:, lo:lo + 2048])
                x_raw.append(tile4)

        for k in range(1, 4):
            load_weights(k)

        w_grouped = {}

        def regroup(k, g, engine, lo=0, cols=BANK):
            if lo == 0:
                w_grouped[(k, g)] = grp.tile([P, 2048], BF16, name="w_grouped%d%d" % (k, g), tag="grp", align_bytes=64)
            dst = w_grouped[(k, g)][:, 4 * lo:4 * (lo + cols)].rearrange("q (c i t) -> q c t i", i=4, t=4)
            src = w_raw[k][:, g * 2048:(g + 1) * 2048].rearrange("q (t n) -> q t n", t=4)
            src = src[:, :, lo:lo + cols].rearrange("q t (c i) -> q c t i", i=4)
            if engine == "S":
                nc.scalar.copy(out=dst, in_=src)
            else:
                nc.vector.tensor_copy(out=dst, in_=src)

        def quantise_w(k, g, lo=0, cols=BANK):
            nh, gate, part = blocks[k]
            at = (gate * 4 + part * 2 + g) * 1024 + nh * BANK + lo
            nc.vector.quantize_mx(
                out=w_codes[:, at:at + cols].bitcast(FP8X4),
                scales=w_scales[:, at:at + cols],
                in_=w_grouped[(k, g)][:, 4 * lo:4 * (lo + cols)],
            )

        for g in range(2):
            regroup(0, g, "V")
        for g in range(2):
            quantise_w(0, g)

        x_grouped = {}

        def transpose_pair(si, tp):
            words = x_raw[si * 2 + tp // 2][:].bitcast(F32)
            h = tp // 2
            for g in range(2):
                bank = psum.tile([P, BANK], F32, name="bank_x", tag="bank")
                for u in range(2):
                    for t2 in range(2):
                        w0 = ((tp % 2) * 2 + t2) * 512 + 2 * g * P
                        o0 = (u * 2 + t2) * P
                        nc.tensor.transpose(bank[:, o0:o0 + P], words[:, w0 + u:w0 + 2 * P:2], ident[:])
                c = 2 * si + g
                if tp % 2 == 0:
                    x_grouped[(c, h)] = grp.tile([P, 2048], BF16, name="x_grouped%d%d" % (c, h), tag="grp", align_bytes=64)
                dst = x_grouped[(c, h)][:].bitcast(F32).rearrange("q (c u) -> q c u", u=2)
                dst = dst[:, (tp % 2) * 256:(tp % 2) * 256 + 256, :]
                src = bank[:].rearrange("q (u c) -> q c u", u=2)
                if (si * 8 + tp * 2 + g) in VECTOR_X_BANKS:
                    nc.vector.tensor_copy(out=dst, in_=src)
                else:
                    nc.scalar.copy(out=dst, in_=src)

        def quantise_x(si, h):
            for g in range(2):
                c = 2 * si + g
                lo = c * 1024 + h * BANK
                nc.vector.quantize_mx(
                    out=x_codes[:, lo:lo + BANK].bitcast(FP8X4),
                    scales=x_scales[:, lo:lo + BANK],
                    in_=x_grouped[(c, h)][:],
                )

        def biases():
            bank = psum.tile([P, BANK], F32, name="bank_b", tag="bank")
            for col in range(8):
                lo = (col // 4) * 1024 + (col % 4) * P
                nc.tensor.matmul(bank[:, col * 32:(col + 1) * 32], lhsT=bias_row[:, lo:lo + P], rhs=ones[:, 0:32],
                                 start=True, stop=True)
            nc.scalar.copy(out=bias_col[:], in_=bank[:, 0:256].rearrange("p (c r) -> p c r", r=32)[:, :, 0])
            for gate in range(2):
                bank = psum.tile([P, BANK], F32, name="bank_w", tag="bank")
                lo = gate * 1024 + BANK
                nc.tensor.matmul(bank[:], lhsT=ones[:], rhs=bias_row[:, lo:lo + BANK], start=True, stop=True)
                nc.scalar.copy(out=bias_wide[:, gate * BANK:(gate + 1) * BANK], in_=bank[:])

        for si in range(2):
            if si == 1:
                biases()
            for tp in range(4):
                transpose_pair(si, tp)
                if (si, tp) in ((0, 2), (1, 0), (1, 2)):
                    done = si * 4 + tp - 2
                    quantise_x(done // 4, (done % 4) // 2)

        for k in range(4, 8):
            load_weights(k)

        banks = {}
        sigmoids = {}
        sums = {}
        gate_out = {}
        staged = {}

        def mx_pass(nh, gate, h, i, lo, cols, c):
            w_at = (gate * 4 + c) * 1024 + nh * BANK
            if nh == 0:
                l_at, r_at = w_at + i * P, c * 1024 + h * BANK
                l_codes, l_scales, r_codes, r_scales = w_codes, w_scales, x_codes, x_scales
            else:
                l_at, r_at = c * 1024 + (h * 4 + i) * P, w_at + lo
                l_codes, l_scales, r_codes, r_scales = x_codes, x_scales, w_codes, w_scales
            nc.tensor.matmul_mx(
                out=banks[(h, i, lo)][:, 0:cols],
                lhsT=l_codes[:, l_at:l_at + P].bitcast(FP8X4),
                lhsT_scale=l_scales[:, l_at:l_at + P],
                rhs=r_codes[:, r_at:r_at + cols].bitcast(FP8X4),
                rhs_scale=r_scales[:, r_at:r_at + cols],
                start=(c == 0),
                stop=(c == 3),
            )

        def store(nh, h, first, count, lo=0, cols=BANK):
            nc.sync.dma_start(
                out=out_rows[:, h * 4 + first:h * 4 + first + count, nh * BANK + lo:nh * BANK + lo + cols],
                in_=staged[h][:, first:first + count, lo:lo + cols],
            )

        def gate_tile(gate, h, i, lo):
            if gate == 0:
                sigmoids[(h, i)] = spool.tile([P, BANK], F32, name="sigmoid", tag="s")
                gate_out[(h, i, lo)] = sigmoids[(h, i)]
            else:
                gate_out[(h, i, lo)] = gpool.tile([P, BANK], F32, name="tanh", tag="gt")

        def step_1(nh, gate, h, i, lo, cols):
            bank = banks[(h, i, lo)]
            if nh == 0:
                gate_tile(gate, h, i, lo)
                nc.scalar.activation(out=gate_out[(h, i, lo)][:], in_=bank[:], func=ACT.Sigmoid if gate == 0 else ACT.Tanh,
                                     bias=bias_col[:, 4 * gate + i:4 * gate + i + 1])
            else:
                at = gate * BANK + lo
                sums[(h, i, lo)] = upool.tile([P, BANK], F32, name="sum", tag="u")
                nc.vector.tensor_tensor(out=sums[(h, i, lo)][:, 0:cols], in0=bank[:, 0:cols],
                                        in1=bias_wide[:, at:at + cols], op=ALU.add)

        def step_2(nh, gate, h, i, lo, cols):
            if nh == 0:
                product = sigmoids[(h, i)]
                nc.vector.tensor_tensor(out=product[:], in0=product[:], in1=gate_out[(h, i, lo)][:], op=ALU.mult)
            else:
                gate_tile(gate, h, i, lo)
                nc.scalar.activation(out=gate_out[(h, i, lo)][:, 0:cols], in_=sums[(h, i, lo)][:, 0:cols],
                                     func=ACT.Sigmoid if gate == 0 else ACT.Tanh)

        def step_3(nh, gate, h, i, lo, cols):
            engine = nc.gpsimd if h * 4 + i < GPSIMD_PRODUCTS else nc.vector
            engine.tensor_tensor(out=staged[h][:, i, lo:lo + cols], in0=sigmoids[(h, i)][:, lo:lo + cols],
                                 in1=gate_out[(h, i, lo)][:, 0:cols], op=ALU.mult)
            store(nh, h, i, 1, lo, cols)

        def turn_back(nh, h):
            for tl in range(4):
                bank = psum.tile([P, BANK], F32, name="bank_t", tag="bank")
                for i in range(4):
                    nc.tensor.transpose(bank[:, i * P:(i + 1) * P], sigmoids[(h, i)][:, tl * P:(tl + 1) * P], ident[:])
                if tl == VECTOR_BACK_BANK:
                    nc.vector.tensor_copy(out=staged[h][:, tl, :], in_=bank[:])
                else:
                    nc.scalar.copy(out=staged[h][:, tl, :], in_=bank[:])
                if tl % 2 == 1:
                    store(nh, h, tl - 1, 2)

        pairs = [(h, i) for h in range(2) for i in range(4)]
        visits = []
        for nh in range(2):
            for gate in range(2):
                if nh == 0:
                    for part in range(2):
                        for h, i in pairs:
                            visits.append(((nh, gate, h, i, 0, BANK), (2 * part, 2 * part + 1)))
                else:
                    for h, i in pairs:
                        if gate == 1 and h * 4 + i >= 8 - HALVED_GROUPS:
                            visits.append(((nh, gate, h, i, 0, 256), (0, 1, 2, 3)))
                            visits.append(((nh, gate, h, i, 256, 256), (0, 1, 2, 3)))
                        else:
                            visits.append(((nh, gate, h, i, 0, BANK), (0, 1, 2, 3)))
        later = {}

        def defer(n, step, args):
            later[n] = later.get(n, []) + [(step, args)]

        quantise_x(1, 1)

        sub_blocks = [(k, g) for k in range(1, 8) for g in range(2)]
        for n in range(len(visits) + TURN_BACK_LAG + 1):
            for k, g in sub_blocks:
                if REGROUP_AT[(k, g)][0] == n:
                    if REGROUP_AT[(k, g)][1] == "VS":
                        regroup(k, g, "V", 0, VECTOR_SHARE)
                        regroup(k, g, "S", VECTOR_SHARE, BANK - VECTOR_SHARE)
                    else:
                        regroup(k, g, REGROUP_AT[(k, g)][1])
            for k, g in sub_blocks:
                if QUANT_AT[(k, g)] == n:
                    quantise_w(k, g)
            if n < len(visits):
                group, passes = visits[n]
                nh, gate, h, i, lo, cols = group
                if passes == (0, 1):
                    if (h, i) == (0, 0):
                        for h2, i2 in pairs:
                            banks[(h2, i2, 0)] = psum.tile([P, BANK], F32, name="bank_g", tag="bank")
                        for c in passes:
                            for h2, i2 in sorted(pairs, key=lambda hi: hi[1] // 2):
                                mx_pass(nh, gate, h2, i2, 0, BANK, c)
                else:
                    if passes[0] == 0:
                        banks[(h, i, lo)] = psum.tile([P, BANK], F32, name="bank_g", tag="bank")
                    if gate == 1 and i == 0:
                        staged[h] = stpool.tile([P, 4, BANK], F32, name="staged", tag="st")
                    for c in passes:
                        mx_pass(nh, gate, h, i, lo, cols, c)
                    step_1(*group)
                    if nh == 1 or gate == 1:
                        defer(n + STEP_2_LAG, step_2, group)
                    if nh == 1 and gate == 1:
                        defer(n + STEP_3_LAG, step_3, group)
                    if nh == 0 and gate == 1 and i == 3:
                        defer(n + TURN_BACK_LAG, turn_back, (nh, h))
            for step, args in later.get(n, []):
                step(*args)
